import numpy as np
import ml_dtypes


def mxq(x, axis, fmt="e4m3"):
    dtype, down = {"e4m3": (ml_dtypes.float8_e4m3fn, 7), "e5m2": (ml_dtypes.float8_e5m2, 14)}[fmt]
    v = np.moveaxis(np.asarray(x, np.float32).astype(ml_dtypes.bfloat16).astype(np.float64), axis, -1)
    blocks = v.reshape(v.shape[:-1] + (-1, 32))
    amax = np.abs(blocks).max(-1, keepdims=True)
    byte = np.maximum(np.where(amax > 0, np.frexp(amax)[1] - 1 + 127, 0) - down, 1)
    scale = np.exp2(byte - 127.0)
    codes = (blocks / scale).astype(np.float32).astype(dtype).astype(np.float64)
    return np.moveaxis((codes * scale).reshape(v.shape), -1, axis)


WIDE = False


def mx_kscale(k):
    if not WIDE:
        return np.ones(k)
    levels = np.array([10, -10, 5, -5, 0])
    a = np.random.permutation(np.resize(levels, k // 512 * 4)).reshape(k // 512, 4)
    idx = np.arange(k)
    return np.exp2(a[idx // 512, idx % 128 // 32])


BF16 = ml_dtypes.bfloat16


def bf(x):
    return np.asarray(x, np.float32).astype(BF16)


def f64(x):
    return np.asarray(x).astype(np.float64)


HI, WS, D, F, NH = 64, 4, 512, 2048, 8
EPS = 1e-5
N = HI * HI
NWS = HI // WS
NW = NWS * NWS
NPW = WS * WS
HD = D // NH
SH = WS // 2


def layer_norm(x, g, b):
    m = x.mean(-1, keepdims=True)
    v = ((x - m) ** 2).mean(-1, keepdims=True)
    return (x - m) / np.sqrt(v + EPS) * g + b


def win_part(img):
    return img.reshape(NWS, WS, NWS, WS, D).swapaxes(1, 2).reshape(NW, NPW, D)


def win_merge(win):
    return win.reshape(NWS, NWS, WS, WS, D).swapaxes(1, 2).reshape(HI, HI, D)


def heads(t):
    return np.ascontiguousarray(t.reshape(NW, NPW, NH, HD).swapaxes(1, 2))


def setup_inputs():
    s = mx_kscale(D)
    return {"x_win": bf(np.random.standard_normal((N, D)) * 1.5),
            "ln3_g": bf((1.0 + 0.1 * np.random.standard_normal(D)) * s),
            "ln3_b": bf(0.1 * np.random.standard_normal(D) * s),
            "qkv2_w": bf(np.random.standard_normal((D, 3 * D)) / np.sqrt(D) / s[:, None]),
            "qkv2_b": bf(0.1 * np.random.standard_normal(3 * D))}


def reference(x_win, ln3_g, ln3_b, qkv2_w, qkv2_b):
    h = layer_norm(f64(x_win), f64(ln3_g), f64(ln3_b))
    img = win_merge(h.reshape(NW, NPW, D))
    shifted = win_part(np.roll(img, (-SH, -SH), (0, 1))).reshape(N, D)
    qkv = (mxq(shifted, 1, "e4m3") @ mxq(f64(qkv2_w), 0, "e4m3")) + f64(qkv2_b)
    q, k, v = np.split(qkv, 3, axis=-1)
    return heads(q), heads(k), heads(v)

@@ -1,0 +1,241 @@
+from contextlib import ExitStack
+
+import concourse.mybir as mybir
+from concourse.masks import make_identity
+
+F32 = mybir.dt.float32
+BF16 = mybir.dt.bfloat16
+U32 = mybir.dt.uint32
+U8 = mybir.dt.uint8
+FP8X4 = mybir.dt.float8_e4m3fn_x4
+ALU = mybir.AluOpType
+ACT = mybir.ActivationFunctionType
+
+P = 128
+D = 512
+PACK = 4
+NWS = 16
+NW = NWS * NWS
+WS = 4
+NPW = WS * WS
+SH = WS // 2
+NH = 8
+HD = 64
+GROUPS = NW // P
+BLOCK = 128
+HEADS_PER_BLOCK = BLOCK // HD
+BLOCKS = 3 * D // BLOCK
+ROWS_PER_STAGE = 2
+EPS = 1e-5
+
+FLOPS = 2 * NW * NPW * D * 3 * D
+
+
+def tile_swintransformerblock_pa_t_kernel(
+    tc, x_win, ln3_g, ln3_b, qkv2_w, qkv2_b, out_0, out_1, out_2
+):
+    nc = tc.nc
+    outs = (out_0, out_1, out_2)
+    x_view = x_win.rearrange("(w p) d -> w p d", p=NPW)
+    w_view = qkv2_w.rearrange("(t q) n -> q t n", t=PACK)
+
+    with ExitStack() as ctx:
+        const = ctx.enter_context(tc.tile_pool(name="const", bufs=1))
+        keep = ctx.enter_context(tc.tile_pool(name="keep", bufs=1))
+        small = ctx.enter_context(tc.tile_pool(name="small", bufs=3))
+        work = ctx.enter_context(tc.tile_pool(name="work", bufs=2))
+        zpool = ctx.enter_context(tc.tile_pool(name="zpool", bufs=8))
+        psum_t = ctx.enter_context(tc.psum_pool(name="psum_t", bufs=4))
+        psum_o = ctx.enter_context(tc.psum_pool(name="psum_o", bufs=4))
+
+        stages = [
+            (g, r0)
+            for g in range(GROUPS)
+            for r0 in range(0, WS, ROWS_PER_STAGE)
+        ]
+
+        x_tiles = {}
+
+        def load_x(g, pi):
+            src_pi = (pi + SH) % WS
+            first = (P * g + (NWS if pi >= WS - SH else 0)) % NW
+            head = min(P, NW - first)
+            x_c = keep.tile([P, WS, D], BF16, name="x_%d_%d" % (g, pi))
+            cols = slice(WS * src_pi, WS * src_pi + WS)
+            nc.sync.dma_start(out=x_c[0:head], in_=x_view[first : first + head, cols, :])
+            if head < P:
+                nc.sync.dma_start(out=x_c[head:P], in_=x_view[0 : P - head, cols, :])
+            x_tiles[(g, pi)] = x_c
+
+        w_raw = keep.tile([P, PACK, 3 * D], BF16, name="w_raw")
+
+        def load_w(s):
+            cols = slice(D * s, D * s + D)
+            nc.sync.dma_start(out=w_raw[:, :, cols], in_=w_view[:, :, cols])
+
+        gb_rows = const.tile([P, P], BF16, name="gb_rows")
+        nc.vector.memset(gb_rows[:], 0.0)
+        nc.scalar.dma_start(
+            out=gb_rows[0:PACK, :], in_=ln3_g.rearrange("(t q) -> t q", t=PACK)
+        )
+        nc.scalar.dma_start(
+            out=gb_rows[PACK : 2 * PACK, :], in_=ln3_b.rearrange("(t q) -> t q", t=PACK)
+        )
+        bias_bc = const.tile([P, 3 * D], BF16, name="bias_bc")
+
+        load_x(0, 0)
+        load_x(0, 1)
+        load_w(0)
+        load_x(0, 2)
+        load_x(0, 3)
+        load_w(1)
+        load_w(2)
+        nc.scalar.dma_start(out=bias_bc[:], in_=qkv2_b.partition_broadcast(P))
+        for pi in range(WS):
+            load_x(1, pi)
+
+        ident = const.tile([P, P], F32, name="ident")
+        make_identity(nc, ident[:])
+        ident_bf = const.tile([P, P], BF16, name="ident_bf")
+        nc.vector.tensor_copy(out=ident_bf[:], in_=ident[:])
+        rot = const.tile([P, P], F32, name="rot")
+        ident_rows = ident[:].rearrange("k (a b) -> k a b", b=NWS)
+        rot_rows = rot[:].rearrange("k (a b) -> k a b", b=NWS)
+        nc.vector.tensor_copy(out=rot_rows[:, :, 0 : NWS - 1], in_=ident_rows[:, :, 1:NWS])
+        nc.vector.tensor_copy(out=rot_rows[:, :, NWS - 1 : NWS], in_=ident_rows[:, :, 0:1])
+        eps = const.tile([P, 1], F32, name="eps")
+        nc.vector.memset(eps[:], EPS)
+
+        gb_t = psum_t.tile([P, P], BF16, tag="xt")
+        nc.tensor.transpose(gb_t[:], gb_rows[:], ident_bf[:])
+        gb = const.tile([P, 2 * PACK], F32, name="gb")
+        nc.vector.tensor_copy(out=gb[:], in_=gb_t[:, 0 : 2 * PACK])
+
+        w_grouped = keep.tile([P, 3 * D, PACK], BF16, name="w_grouped", align_bytes=64)
+        w_codes = keep.tile([P, 3 * D], U32, name="w_codes", align_bytes=64)
+        w_scales = keep.tile([P, 3 * D], U8, name="w_scales", align_bytes=64)
+
+        def quantise_w(s):
+            cols = slice(D * s, D * s + D)
+            nc.vector.tensor_copy(
+                out=w_grouped[:, cols, :].rearrange("q (c i) t -> q c t i", i=4),
+                in_=w_raw[:, :, cols].rearrange("q t (c i) -> q c t i", i=4),
+            )
+            nc.vector.quantize_mx(
+                out=w_codes[:, cols].bitcast(FP8X4),
+                scales=w_scales[:, cols],
+                in_=w_grouped[:, cols, :].rearrange("q n t -> q (n t)"),
+            )
+
+        a_codes = {}
+        a_scales = {}
+
+        def layer_norm(g, pi):
+            x_c = x_tiles[(g, pi)]
+            stats = small.tile([P, WS, 6], F32, name="stats")
+            mv = small.tile([P, WS, 2], F32, name="mv")
+            for j in range(WS):
+                nc.vector.bn_stats(out=stats[:, j, :], in_=x_c[:, j, :])
+                nc.vector.bn_aggr(out=mv[:, j, :], in_=stats[:, j, :])
+            std = small.tile([P, WS, 1], F32, name="std")
+            nc.scalar.activation(
+                out=std[:], in_=mv[:, :, 1:2], func=ACT.Sqrt, bias=eps[:], scale=1.0
+            )
+            rstd = small.tile([P, WS, 1], F32, name="rstd")
+            nc.vector.reciprocal(out=rstd[:], in_=std[:])
+            xn = work.tile([P, WS, D], F32, name="xn")
+            for j in range(WS):
+                nc.gpsimd.tensor_scalar(
+                    out=xn[:, j, :],
+                    in0=x_c[:, j, :],
+                    scalar1=mv[:, j, 0:1],
+                    scalar2=rstd[:, j, :],
+                    op0=ALU.subtract,
+                    op1=ALU.mult,
+                )
+            planes = work.tile([P, PACK, WS * P], BF16, name="planes")
+            for t in range(PACK):
+                xt = psum_t.tile([P, WS, P], F32, name="xt")
+                for j in range(WS):
+                    pj = (j + SH) % WS
+                    perm = rot if j < SH else ident
+                    nc.tensor.transpose(xt[:, pj, :], xn[:, j, P * t : P * t + P], perm[:])
+                nc.scalar.activation(
+                    out=planes[:, t, :],
+                    in_=xt[:].rearrange("q j m -> q (j m)"),
+                    func=ACT.Identity,
+                    scale=gb[:, t : t + 1],
+                    bias=gb[:, PACK + t : PACK + t + 1],
+                )
+            grouped = work.tile([P, WS * P, PACK], BF16, name="grouped", align_bytes=64)
+            nc.scalar.copy(
+                out=grouped[:].rearrange("q (c i) t -> q c t i", i=4),
+                in_=planes[:].rearrange("q t (c i) -> q c t i", i=4),
+            )
+            codes = keep.tile([P, WS * P], U32, name="codes_%d_%d" % (g, pi), align_bytes=64)
+            scales = keep.tile([P, WS * P], U8, name="scales_%d_%d" % (g, pi), align_bytes=64)
+            nc.vector.quantize_mx(
+                out=codes[:].bitcast(FP8X4),
+                scales=scales[:],
+                in_=grouped[:].rearrange("q m t -> q (m t)"),
+            )
+            a_codes[(g, pi)] = codes
+            a_scales[(g, pi)] = scales
+
+        banks = [0]
+
+        def project(g, r0, blk):
+            cols = slice(BLOCK * blk, BLOCK * blk + BLOCK)
+            bias_view = (
+                bias_bc[:, cols]
+                .rearrange("m (n o c) -> m n o c", n=HEADS_PER_BLOCK, o=1)
+                .to_broadcast([P, HEADS_PER_BLOCK, WS, HD])
+            )
+            z = zpool.tile([P, HEADS_PER_BLOCK, ROWS_PER_STAGE * WS, HD], F32, name="z")
+            for r in range(ROWS_PER_STAGE):
+                pi = r0 + r
+                acc = psum_o.tile([P, WS, BLOCK], F32, name="acc")
+                for pj in range(WS):
+                    toks = slice(P * pj, P * pj + P)
+                    nc.tensor.matmul_mx(
+                        out=acc[:, pj, :],
+                        lhsT=a_codes[(g, pi)][:, toks].bitcast(FP8X4),
+                        lhsT_scale=a_scales[(g, pi)][:, toks],
+                        rhs=w_codes[:, cols].bitcast(FP8X4),
+                        rhs_scale=w_scales[:, cols],
+                        start=True,
+                        stop=True,
+                    )
+                acc_view = acc[:].rearrange("m p (n c) -> m n p c", n=HEADS_PER_BLOCK)
+                z_part = z[:, :, WS * r : WS * r + WS, :]
+                if banks[0] % 3 == 2:
+                    nc.scalar.copy(out=z_part, in_=acc_view)
+                    nc.gpsimd.tensor_tensor(out=z_part, in0=z_part, in1=bias_view, op=ALU.add)
+                else:
+                    nc.vector.tensor_tensor(out=z_part, in0=acc_view, in1=bias_view, op=ALU.add)
+                banks[0] += 1
+            which = blk // (D // BLOCK)
+            h0 = HEADS_PER_BLOCK * (blk % (D // BLOCK))
+            nc.sync.dma_start(
+                out=outs[which][
+                    P * g : P * g + P,
+                    h0 : h0 + HEADS_PER_BLOCK,
+                    WS * r0 : WS * (r0 + ROWS_PER_STAGE),
+                    :,
+                ],
+                in_=z[:],
+            )
+
+        g0, first_row = stages[0]
+        for r in range(ROWS_PER_STAGE):
+            layer_norm(g0, first_row + r)
+        quantise_w(0)
+        every = BLOCKS // ROWS_PER_STAGE
+        for s, (g, r0) in enumerate(stages):
+            for blk in range(BLOCKS):
+                if s == 0 and blk in (1, 2):
+                    quantise_w(blk)
+                if s + 1 < len(stages) and blk % every == 0:
+                    g_next, r_next = stages[s + 1]
+                    layer_norm(g_next, r_next + blk // every)
+                project(g, r0, blk)

@@ -19,14 +19,19 @@ NW = NWS * NWS
 WS = 4
 NPW = WS * WS
 SH = WS // 2
-NH = 8
 HD = 64
 GROUPS = NW // P
 BLOCK = 128
 HEADS_PER_BLOCK = BLOCK // HD
 BLOCKS = 3 * D // BLOCK
-ROWS_PER_STAGE = 2
+BLOCKS_PER_OUT = D // BLOCK
+BANKS_PER_STORE = 2
 EPS = 1e-5
+
+CHUNKS = [(g, row) for g in range(GROUPS) for row in range(WS)]
+STAGES = [CHUNKS[0:1], CHUNKS[1:2], CHUNKS[2:4], CHUNKS[4:6], CHUNKS[6:8]]
+SCALAR_STATS = CHUNKS[4:8]
+VECTOR_REGROUPS = CHUNKS[0:2]
 
 FLOPS = 2 * NW * NPW * D * 3 * D
 
@@ -42,30 +47,25 @@ def tile_swintransformerblock_pa_t_kernel(
     with ExitStack() as ctx:
         const = ctx.enter_context(tc.tile_pool(name="const", bufs=1))
         keep = ctx.enter_context(tc.tile_pool(name="keep", bufs=1))
-        small = ctx.enter_context(tc.tile_pool(name="small", bufs=3))
+        small = ctx.enter_context(tc.tile_pool(name="small", bufs=4))
         work = ctx.enter_context(tc.tile_pool(name="work", bufs=2))
         zpool = ctx.enter_context(tc.tile_pool(name="zpool", bufs=8))
         psum_t = ctx.enter_context(tc.psum_pool(name="psum_t", bufs=4))
         psum_o = ctx.enter_context(tc.psum_pool(name="psum_o", bufs=4))
 
-        stages = [
-            (g, r0)
-            for g in range(GROUPS)
-            for r0 in range(0, WS, ROWS_PER_STAGE)
-        ]
-
         x_tiles = {}
 
-        def load_x(g, pi):
-            src_pi = (pi + SH) % WS
-            first = (P * g + (NWS if pi >= WS - SH else 0)) % NW
+        def load_x(chunk):
+            g, row = chunk
+            src_row = (row + SH) % WS
+            first = (P * g + (NWS if row >= WS - SH else 0)) % NW
             head = min(P, NW - first)
-            x_c = keep.tile([P, WS, D], BF16, name="x_%d_%d" % (g, pi))
-            cols = slice(WS * src_pi, WS * src_pi + WS)
+            x_c = keep.tile([P, WS, D], BF16, name="x_%d_%d" % chunk)
+            cols = slice(WS * src_row, WS * src_row + WS)
             nc.sync.dma_start(out=x_c[0:head], in_=x_view[first : first + head, cols, :])
             if head < P:
                 nc.sync.dma_start(out=x_c[head:P], in_=x_view[0 : P - head, cols, :])
-            x_tiles[(g, pi)] = x_c
+            x_tiles[chunk] = x_c
 
         w_raw = keep.tile([P, PACK, 3 * D], BF16, name="w_raw")
 
@@ -83,16 +83,16 @@ def tile_swintransformerblock_pa_t_kernel(
         )
         bias_bc = const.tile([P, 3 * D], BF16, name="bias_bc")
 
-        load_x(0, 0)
-        load_x(0, 1)
+        load_x(CHUNKS[0])
+        load_x(CHUNKS[1])
         load_w(0)
-        load_x(0, 2)
-        load_x(0, 3)
+        load_x(CHUNKS[2])
+        load_x(CHUNKS[3])
         load_w(1)
         load_w(2)
         nc.scalar.dma_start(out=bias_bc[:], in_=qkv2_b.partition_broadcast(P))
-        for pi in range(WS):
-            load_x(1, pi)
+        for chunk in CHUNKS[4:]:
+            load_x(chunk)
 
         ident = const.tile([P, P], F32, name="ident")
         make_identity(nc, ident[:])
@@ -117,7 +117,7 @@ def tile_swintransformerblock_pa_t_kernel(
 
         def quantise_w(s):
             cols = slice(D * s, D * s + D)
-            nc.vector.tensor_copy(
+            nc.scalar.copy(
                 out=w_grouped[:, cols, :].rearrange("q (c i) t -> q c t i", i=4),
                 in_=w_raw[:, :, cols].rearrange("q t (c i) -> q c t i", i=4),
             )
@@ -127,32 +127,74 @@ def tile_swintransformerblock_pa_t_kernel(
                 in_=w_grouped[:, cols, :].rearrange("q n t -> q (n t)"),
             )
 
+        scale_of = {}
+        shift_of = {}
+        xn_of = {}
+        planes_of = {}
         a_codes = {}
         a_scales = {}
 
-        def layer_norm(g, pi):
-            x_c = x_tiles[(g, pi)]
-            stats = small.tile([P, WS, 6], F32, name="stats")
-            mv = small.tile([P, WS, 2], F32, name="mv")
-            for j in range(WS):
-                nc.vector.bn_stats(out=stats[:, j, :], in_=x_c[:, j, :])
-                nc.vector.bn_aggr(out=mv[:, j, :], in_=stats[:, j, :])
+        def statistics(chunk):
+            x_c = x_tiles[chunk]
+            negmean = small.tile([P, WS, 1], F32, name="negmean")
             std = small.tile([P, WS, 1], F32, name="std")
-            nc.scalar.activation(
-                out=std[:], in_=mv[:, :, 1:2], func=ACT.Sqrt, bias=eps[:], scale=1.0
-            )
+            if chunk in SCALAR_STATS:
+                sums = small.tile([P, WS, 1], F32, name="sums")
+                squares = small.tile([P, WS, 1], F32, name="squares")
+                unread_a = work.tile([P, WS, D], BF16, name="unread_a")
+                unread_b = work.tile([P, WS, D], BF16, name="unread_b")
+                for j in range(WS):
+                    nc.scalar.activation(
+                        out=unread_a[:, j, :],
+                        in_=x_c[:, j, :],
+                        func=ACT.Identity,
+                        accum_out=sums[:, j, :],
+                    )
+                nc.scalar.mul(out=negmean[:], in_=sums[:], mul=-1.0 / D)
+                for j in range(WS):
+                    nc.scalar.activation(
+                        out=unread_b[:, j, :],
+                        in_=x_c[:, j, :],
+                        func=ACT.Square,
+                        bias=negmean[:, j, :],
+                        scale=1.0,
+                        accum_out=squares[:, j, :],
+                    )
+                nc.scalar.activation(
+                    out=std[:], in_=squares[:], func=ACT.Sqrt, bias=eps[:], scale=1.0 / D
+                )
+            else:
+                stats = small.tile([P, WS, 6], F32, name="stats")
+                mv = small.tile([P, WS, 2], F32, name="mv")
+                for j in range(WS):
+                    nc.vector.bn_stats(out=stats[:, j, :], in_=x_c[:, j, :])
+                    nc.vector.bn_aggr(out=mv[:, j, :], in_=stats[:, j, :])
+                nc.vector.tensor_scalar_mul(out=negmean[:], in0=mv[:, :, 0:1], scalar1=-1.0)
+                nc.scalar.activation(
+                    out=std[:], in_=mv[:, :, 1:2], func=ACT.Sqrt, bias=eps[:], scale=1.0
+                )
             rstd = small.tile([P, WS, 1], F32, name="rstd")
             nc.vector.reciprocal(out=rstd[:], in_=std[:])
+            nmr = small.tile([P, WS, 1], F32, name="nmr")
+            nc.vector.tensor_tensor(out=nmr[:], in0=negmean[:], in1=rstd[:], op=ALU.mult)
+            scale_of[chunk] = rstd
+            shift_of[chunk] = nmr
+
+        def normalise(chunk):
             xn = work.tile([P, WS, D], F32, name="xn")
             for j in range(WS):
                 nc.gpsimd.tensor_scalar(
                     out=xn[:, j, :],
-                    in0=x_c[:, j, :],
-                    scalar1=mv[:, j, 0:1],
-                    scalar2=rstd[:, j, :],
-                    op0=ALU.subtract,
-                    op1=ALU.mult,
+                    in0=x_tiles[chunk][:, j, :],
+                    scalar1=scale_of[chunk][:, j, :],
+                    scalar2=shift_of[chunk][:, j, :],
+                    op0=ALU.mult,
+                    op1=ALU.add,
                 )
+            xn_of[chunk] = xn
+
+        def transpose_and_scale(chunk):
+            xn = xn_of[chunk]
             planes = work.tile([P, PACK, WS * P], BF16, name="planes")
             for t in range(PACK):
                 xt = psum_t.tile([P, WS, P], F32, name="xt")
@@ -167,75 +209,94 @@ def tile_swintransformerblock_pa_t_kernel(
                     scale=gb[:, t : t + 1],
                     bias=gb[:, PACK + t : PACK + t + 1],
                 )
+            planes_of[chunk] = planes
+
+        def regroup_and_quantise(chunk):
             grouped = work.tile([P, WS * P, PACK], BF16, name="grouped", align_bytes=64)
-            nc.scalar.copy(
-                out=grouped[:].rearrange("q (c i) t -> q c t i", i=4),
-                in_=planes[:].rearrange("q t (c i) -> q c t i", i=4),
-            )
-            codes = keep.tile([P, WS * P], U32, name="codes_%d_%d" % (g, pi), align_bytes=64)
-            scales = keep.tile([P, WS * P], U8, name="scales_%d_%d" % (g, pi), align_bytes=64)
+            dst = grouped[:].rearrange("q (c i) t -> q c t i", i=4)
+            src = planes_of[chunk][:].rearrange("q t (c i) -> q c t i", i=4)
+            if chunk in VECTOR_REGROUPS:
+                nc.vector.tensor_copy(out=dst, in_=src)
+            else:
+                nc.scalar.copy(out=dst, in_=src)
+            codes = keep.tile([P, WS * P], U32, name="codes_%d_%d" % chunk, align_bytes=64)
+            scales = keep.tile([P, WS * P], U8, name="scales_%d_%d" % chunk, align_bytes=64)
             nc.vector.quantize_mx(
                 out=codes[:].bitcast(FP8X4),
                 scales=scales[:],
                 in_=grouped[:].rearrange("q m t -> q (m t)"),
             )
-            a_codes[(g, pi)] = codes
-            a_scales[(g, pi)] = scales
+            a_codes[chunk] = codes
+            a_scales[chunk] = scales
 
-        banks = [0]
+        def layer_norm(stage):
+            for chunk in stage:
+                statistics(chunk)
+            for chunk in stage:
+                normalise(chunk)
+                transpose_and_scale(chunk)
+                regroup_and_quantise(chunk)
 
-        def project(g, r0, blk):
-            cols = slice(BLOCK * blk, BLOCK * blk + BLOCK)
-            bias_view = (
-                bias_bc[:, cols]
-                .rearrange("m (n o c) -> m n o c", n=HEADS_PER_BLOCK, o=1)
-                .to_broadcast([P, HEADS_PER_BLOCK, WS, HD])
-            )
-            z = zpool.tile([P, HEADS_PER_BLOCK, ROWS_PER_STAGE * WS, HD], F32, name="z")
-            for r in range(ROWS_PER_STAGE):
-                pi = r0 + r
-                acc = psum_o.tile([P, WS, BLOCK], F32, name="acc")
-                for pj in range(WS):
-                    toks = slice(P * pj, P * pj + P)
-                    nc.tensor.matmul_mx(
-                        out=acc[:, pj, :],
-                        lhsT=a_codes[(g, pi)][:, toks].bitcast(FP8X4),
-                        lhsT_scale=a_scales[(g, pi)][:, toks],
-                        rhs=w_codes[:, cols].bitcast(FP8X4),
-                        rhs_scale=w_scales[:, cols],
-                        start=True,
-                        stop=True,
+        def project(stage):
+            rows = len(stage)
+            g, row0 = stage[0]
+            blocks_per_store = BANKS_PER_STORE // rows
+            heads = HEADS_PER_BLOCK * blocks_per_store
+            for blk0 in range(0, BLOCKS, blocks_per_store):
+                z = zpool.tile([P, heads, rows * WS, HD], F32, name="z", tag="z")
+                for b in range(blocks_per_store):
+                    cols = slice(BLOCK * (blk0 + b), BLOCK * (blk0 + b) + BLOCK)
+                    bias_view = (
+                        bias_bc[:, cols]
+                        .rearrange("m (n o c) -> m n o c", n=HEADS_PER_BLOCK, o=1)
+                        .to_broadcast([P, HEADS_PER_BLOCK, WS, HD])
                     )
-                acc_view = acc[:].rearrange("m p (n c) -> m n p c", n=HEADS_PER_BLOCK)
-                z_part = z[:, :, WS * r : WS * r + WS, :]
-                if banks[0] % 3 == 2:
-                    nc.scalar.copy(out=z_part, in_=acc_view)
-                    nc.gpsimd.tensor_tensor(out=z_part, in0=z_part, in1=bias_view, op=ALU.add)
-                else:
-                    nc.vector.tensor_tensor(out=z_part, in0=acc_view, in1=bias_view, op=ALU.add)
-                banks[0] += 1
-            which = blk // (D // BLOCK)
-            h0 = HEADS_PER_BLOCK * (blk % (D // BLOCK))
-            nc.sync.dma_start(
-                out=outs[which][
-                    P * g : P * g + P,
-                    h0 : h0 + HEADS_PER_BLOCK,
-                    WS * r0 : WS * (r0 + ROWS_PER_STAGE),
-                    :,
-                ],
-                in_=z[:],
-            )
+                    for r, chunk in enumerate(stage):
+                        acc = psum_o.tile([P, WS, BLOCK], F32, name="acc")
+                        for pj in range(WS):
+                            toks = slice(P * pj, P * pj + P)
+                            nc.tensor.matmul_mx(
+                                out=acc[:, pj, :],
+                                lhsT=a_codes[chunk][:, toks].bitcast(FP8X4),
+                                lhsT_scale=a_scales[chunk][:, toks],
+                                rhs=w_codes[:, cols].bitcast(FP8X4),
+                                rhs_scale=w_scales[:, cols],
+                                start=True,
+                                stop=True,
+                            )
+                        nc.vector.tensor_tensor(
+                            out=z[
+                                :,
+                                HEADS_PER_BLOCK * b : HEADS_PER_BLOCK * (b + 1),
+                                WS * r : WS * r + WS,
+                                :,
+                            ],
+                            in0=acc[:].rearrange("m p (n c) -> m n p c", n=HEADS_PER_BLOCK),
+                            in1=bias_view,
+                            op=ALU.add,
+                        )
+                which = blk0 // BLOCKS_PER_OUT
+                h0 = HEADS_PER_BLOCK * (blk0 % BLOCKS_PER_OUT)
+                nc.sync.dma_start(
+                    out=outs[which][
+                        P * g : P * g + P,
+                        h0 : h0 + heads,
+                        WS * row0 : WS * (row0 + rows),
+                        :,
+                    ],
+                    in_=z[:],
+                )
 
-        g0, first_row = stages[0]
-        for r in range(ROWS_PER_STAGE):
-            layer_norm(g0, first_row + r)
+        layer_norm(STAGES[0])
         quantise_w(0)
-        every = BLOCKS // ROWS_PER_STAGE
-        for s, (g, r0) in enumerate(stages):
-            for blk in range(BLOCKS):
-                if s == 0 and blk in (1, 2):
-                    quantise_w(blk)
-                if s + 1 < len(stages) and blk % every == 0:
-                    g_next, r_next = stages[s + 1]
-                    layer_norm(g_next, r_next + blk // every)
-                project(g, r0, blk)
+        layer_norm(STAGES[1])
+        quantise_w(1)
+        quantise_w(2)
+        layer_norm(STAGES[2])
+        project(STAGES[0])
+        project(STAGES[1])
+        layer_norm(STAGES[3])
+        project(STAGES[2])
+        layer_norm(STAGES[4])
+        project(STAGES[3])
+        project(STAGES[4])

@@ -30,8 +30,9 @@ EPS = 1e-5
 
 CHUNKS = [(g, row) for g in range(GROUPS) for row in range(WS)]
 STAGES = [CHUNKS[0:1], CHUNKS[1:2], CHUNKS[2:4], CHUNKS[4:6], CHUNKS[6:8]]
-SCALAR_STATS = CHUNKS[4:8]
+SCALAR_STATS = CHUNKS[3::2]
 VECTOR_REGROUPS = CHUNKS[0:2]
+VECTOR_NORMALISES = CHUNKS[0:1]
 
 FLOPS = 2 * NW * NPW * D * 3 * D
 
@@ -90,7 +91,7 @@ def tile_swintransformerblock_pa_t_kernel(
         load_x(CHUNKS[3])
         load_w(1)
         load_w(2)
-        nc.scalar.dma_start(out=bias_bc[:], in_=qkv2_b.partition_broadcast(P))
+        nc.sync.dma_start(out=bias_bc[:], in_=qkv2_b.partition_broadcast(P))
         for chunk in CHUNKS[4:]:
             load_x(chunk)
 
@@ -105,6 +106,8 @@ def tile_swintransformerblock_pa_t_kernel(
         nc.vector.tensor_copy(out=rot_rows[:, :, NWS - 1 : NWS], in_=ident_rows[:, :, 0:1])
         eps = const.tile([P, 1], F32, name="eps")
         nc.vector.memset(eps[:], EPS)
+        warm = const.tile([P, 1], F32, name="warm")
+        nc.scalar.activation(out=warm[:], in_=eps[:], func=ACT.Sqrt)
 
         gb_t = psum_t.tile([P, P], BF16, tag="xt")
         nc.tensor.transpose(gb_t[:], gb_rows[:], ident_bf[:])
@@ -182,8 +185,9 @@ def tile_swintransformerblock_pa_t_kernel(
 
         def normalise(chunk):
             xn = work.tile([P, WS, D], F32, name="xn")
+            engine = nc.vector if chunk in VECTOR_NORMALISES else nc.gpsimd
             for j in range(WS):
-                nc.gpsimd.tensor_scalar(
+                engine.tensor_scalar(
                     out=xn[:, j, :],
                     in0=x_tiles[chunk][:, j, :],
                     scalar1=scale_of[chunk][:, j, :],
@@ -294,9 +298,9 @@ def tile_swintransformerblock_pa_t_kernel(
         quantise_w(2)
         layer_norm(STAGES[2])
         project(STAGES[0])
-        project(STAGES[1])
         layer_norm(STAGES[3])
-        project(STAGES[2])
+        project(STAGES[1])
         layer_norm(STAGES[4])
+        project(STAGES[2])
         project(STAGES[3])
         project(STAGES[4])

@@ -32,7 +32,7 @@ CHUNKS = [(g, row) for g in range(GROUPS) for row in range(WS)]
 STAGES = [CHUNKS[0:1], CHUNKS[1:2], CHUNKS[2:4], CHUNKS[4:6], CHUNKS[6:8]]
 SCALAR_STATS = CHUNKS[3::2]
 VECTOR_REGROUPS = CHUNKS[0:2]
-VECTOR_NORMALISES = CHUNKS[0:1]
+VECTOR_NORMALISES = CHUNKS
 
 FLOPS = 2 * NW * NPW * D * 3 * D
 

@@ -29,10 +29,10 @@ BANKS_PER_STORE = 2
 EPS = 1e-5
 
 CHUNKS = [(g, row) for g in range(GROUPS) for row in range(WS)]
-STAGES = [CHUNKS[0:1], CHUNKS[1:2], CHUNKS[2:4], CHUNKS[4:6], CHUNKS[6:8]]
-SCALAR_STATS = CHUNKS[3::2]
-VECTOR_REGROUPS = CHUNKS[0:2]
-VECTOR_NORMALISES = CHUNKS
+STAGES = [CHUNKS[0:1], CHUNKS[1:2], CHUNKS[2:4], CHUNKS[4:6], CHUNKS[6:7], CHUNKS[7:8]]
+SCALAR_STATS = [CHUNKS[2], CHUNKS[4], CHUNKS[6], CHUNKS[7]]
+VECTOR_REGROUPS = CHUNKS[0:1]
+VECTOR_NORMALISES = CHUNKS[0:4]
 
 FLOPS = 2 * NW * NPW * D * 3 * D
 
@@ -120,10 +120,16 @@ def tile_swintransformerblock_pa_t_kernel(
 
         def quantise_w(s):
             cols = slice(D * s, D * s + D)
-            nc.scalar.copy(
-                out=w_grouped[:, cols, :].rearrange("q (c i) t -> q c t i", i=4),
-                in_=w_raw[:, :, cols].rearrange("q t (c i) -> q c t i", i=4),
-            )
+            for piece in range(4):
+                pc = slice(D * s + P * piece, D * s + P * piece + P)
+                nc.gpsimd.tensor_scalar(
+                    out=w_grouped[:, pc, :],
+                    in0=w_raw[:, :, pc].rearrange("q t n -> q n t"),
+                    scalar1=1.0,
+                    scalar2=0.0,
+                    op0=ALU.mult,
+                    op1=ALU.add,
+                )
             nc.vector.quantize_mx(
                 out=w_codes[:, cols].bitcast(FP8X4),
                 scales=w_scales[:, cols],
@@ -185,16 +191,24 @@ def tile_swintransformerblock_pa_t_kernel(
 
         def normalise(chunk):
             xn = work.tile([P, WS, D], F32, name="xn")
-            engine = nc.vector if chunk in VECTOR_NORMALISES else nc.gpsimd
             for j in range(WS):
-                engine.tensor_scalar(
-                    out=xn[:, j, :],
-                    in0=x_tiles[chunk][:, j, :],
-                    scalar1=scale_of[chunk][:, j, :],
-                    scalar2=shift_of[chunk][:, j, :],
-                    op0=ALU.mult,
-                    op1=ALU.add,
-                )
+                if chunk in VECTOR_NORMALISES:
+                    nc.vector.tensor_scalar(
+                        out=xn[:, j, :],
+                        in0=x_tiles[chunk][:, j, :],
+                        scalar1=scale_of[chunk][:, j, :],
+                        scalar2=shift_of[chunk][:, j, :],
+                        op0=ALU.mult,
+                        op1=ALU.add,
+                    )
+                else:
+                    nc.scalar.activation(
+                        out=xn[:, j, :],
+                        in_=x_tiles[chunk][:, j, :],
+                        func=ACT.Identity,
+                        scale=scale_of[chunk][:, j, :],
+                        bias=shift_of[chunk][:, j, :],
+                    )
             xn_of[chunk] = xn
 
         def transpose_and_scale(chunk):
@@ -297,10 +311,12 @@ def tile_swintransformerblock_pa_t_kernel(
         quantise_w(1)
         quantise_w(2)
         layer_norm(STAGES[2])
-        project(STAGES[0])
         layer_norm(STAGES[3])
-        project(STAGES[1])
+        project(STAGES[0])
         layer_norm(STAGES[4])
+        project(STAGES[1])
+        layer_norm(STAGES[5])
         project(STAGES[2])
         project(STAGES[3])
         project(STAGES[4])
+        project(STAGES[5])

@@ -29,8 +29,8 @@ BANKS_PER_STORE = 2
 EPS = 1e-5
 
 CHUNKS = [(g, row) for g in range(GROUPS) for row in range(WS)]
-STAGES = [CHUNKS[0:1], CHUNKS[1:2], CHUNKS[2:4], CHUNKS[4:6], CHUNKS[6:7], CHUNKS[7:8]]
-SCALAR_STATS = [CHUNKS[2], CHUNKS[4], CHUNKS[6], CHUNKS[7]]
+STAGES = [CHUNKS[0:2], CHUNKS[2:4], CHUNKS[4:6], CHUNKS[6:8]]
+SCALAR_STATS = CHUNKS[3::2]
 VECTOR_REGROUPS = CHUNKS[0:1]
 VECTOR_NORMALISES = CHUNKS[0:4]
 
@@ -311,12 +311,8 @@ def tile_swintransformerblock_pa_t_kernel(
         quantise_w(1)
         quantise_w(2)
         layer_norm(STAGES[2])
-        layer_norm(STAGES[3])
         project(STAGES[0])
-        layer_norm(STAGES[4])
+        layer_norm(STAGES[3])
         project(STAGES[1])
-        layer_norm(STAGES[5])
         project(STAGES[2])
         project(STAGES[3])
-        project(STAGES[4])
-        project(STAGES[5])

@@ -83,6 +83,9 @@ def tile_swintransformerblock_pa_t_kernel(
             out=gb_rows[PACK : 2 * PACK, :], in_=ln3_b.rearrange("(t q) -> t q", t=PACK)
         )
         bias_bc = const.tile([P, 3 * D], BF16, name="bias_bc")
+        bias_row = const.tile([P, 3 * D], BF16, name="bias_row")
+        nc.gpsimd.memset(bias_row[:], 0.0)
+        nc.scalar.dma_start(out=bias_row[0:1, :], in_=qkv2_b.rearrange("(o n) -> o n", o=1))
 
         load_x(CHUNKS[0])
         load_x(CHUNKS[1])
@@ -91,7 +94,6 @@ def tile_swintransformerblock_pa_t_kernel(
         load_x(CHUNKS[3])
         load_w(1)
         load_w(2)
-        nc.sync.dma_start(out=bias_bc[:], in_=qkv2_b.partition_broadcast(P))
         for chunk in CHUNKS[4:]:
             load_x(chunk)
 
@@ -113,6 +115,15 @@ def tile_swintransformerblock_pa_t_kernel(
         nc.tensor.transpose(gb_t[:], gb_rows[:], ident_bf[:])
         gb = const.tile([P, 2 * PACK], F32, name="gb")
         nc.vector.tensor_copy(out=gb[:], in_=gb_t[:, 0 : 2 * PACK])
+
+        ones = const.tile([P, P], BF16, name="ones")
+        nc.vector.memset(ones[:], 1.0)
+        for s in range(3):
+            spread = psum_o.tile([P, D], F32, name="acc")
+            nc.tensor.matmul(
+                spread[:], lhsT=ones[:], rhs=bias_row[:, D * s : D * s + D], start=True, stop=True
+            )
+            nc.scalar.copy(out=bias_bc[:, D * s : D * s + D], in_=spread[:])
 
         w_grouped = keep.tile([P, 3 * D, PACK], BF16, name="w_grouped", align_bytes=64)
         w_codes = keep.tile([P, 3 * D], U32, name="w_codes", align_bytes=64)

from contextlib import ExitStack

import concourse.mybir as mybir
from concourse.masks import make_identity

F32 = mybir.dt.float32
BF16 = mybir.dt.bfloat16
U32 = mybir.dt.uint32
U8 = mybir.dt.uint8
FP8X4 = mybir.dt.float8_e4m3fn_x4
ALU = mybir.AluOpType
ACT = mybir.ActivationFunctionType

P = 128
D = 512
PACK = 4
NWS = 16
NW = NWS * NWS
WS = 4
NPW = WS * WS
SH = WS // 2
HD = 64
GROUPS = NW // P
BLOCK = 128
HEADS_PER_BLOCK = BLOCK // HD
BLOCKS = 3 * D // BLOCK
BLOCKS_PER_OUT = D // BLOCK
BANKS_PER_STORE = 2
EPS = 1e-5

CHUNKS = [(g, row) for g in range(GROUPS) for row in range(WS)]
STAGES = [CHUNKS[0:2], CHUNKS[2:4], CHUNKS[4:6], CHUNKS[6:8]]
SCALAR_STATS = CHUNKS[3::2]
VECTOR_REGROUPS = CHUNKS[0:1]
VECTOR_NORMALISES = CHUNKS[0:4]

FLOPS = 2 * NW * NPW * D * 3 * D


def tile_swintransformerblock_pa_t_kernel(
    tc, x_win, ln3_g, ln3_b, qkv2_w, qkv2_b, out_0, out_1, out_2
):
    nc = tc.nc
    outs = (out_0, out_1, out_2)
    x_view = x_win.rearrange("(w p) d -> w p d", p=NPW)
    w_view = qkv2_w.rearrange("(t q) n -> q t n", t=PACK)

    with ExitStack() as ctx:
        const = ctx.enter_context(tc.tile_pool(name="const", bufs=1))
        keep = ctx.enter_context(tc.tile_pool(name="keep", bufs=1))
        small = ctx.enter_context(tc.tile_pool(name="small", bufs=4))
        work = ctx.enter_context(tc.tile_pool(name="work", bufs=2))
        zpool = ctx.enter_context(tc.tile_pool(name="zpool", bufs=8))
        psum_t = ctx.enter_context(tc.psum_pool(name="psum_t", bufs=4))
        psum_o = ctx.enter_context(tc.psum_pool(name="psum_o", bufs=4))

        x_tiles = {}

        def load_x(chunk):
            g, row = chunk
            src_row = (row + SH) % WS
            first = (P * g + (NWS if row >= WS - SH else 0)) % NW
            head = min(P, NW - first)
            x_c = keep.tile([P, WS, D], BF16, name="x_%d_%d" % chunk)
            cols = slice(WS * src_row, WS * src_row + WS)
            nc.sync.dma_start(out=x_c[0:head], in_=x_view[first : first + head, cols, :])
            if head < P:
                nc.sync.dma_start(out=x_c[head:P], in_=x_view[0 : P - head, cols, :])
            x_tiles[chunk] = x_c

        w_raw = keep.tile([P, PACK, 3 * D], BF16, name="w_raw")

        def load_w(s):
            cols = slice(D * s, D * s + D)
            nc.sync.dma_start(out=w_raw[:, :, cols], in_=w_view[:, :, cols])

        gb_rows = const.tile([P, P], BF16, name="gb_rows")
        nc.vector.memset(gb_rows[:], 0.0)
        nc.scalar.dma_start(
            out=gb_rows[0:PACK, :], in_=ln3_g.rearrange("(t q) -> t q", t=PACK)
        )
        nc.scalar.dma_start(
            out=gb_rows[PACK : 2 * PACK, :], in_=ln3_b.rearrange("(t q) -> t q", t=PACK)
        )
        bias_bc = const.tile([P, 3 * D], BF16, name="bias_bc")
        bias_row = const.tile([P, 3 * D], BF16, name="bias_row")
        nc.gpsimd.memset(bias_row[:], 0.0)
        nc.scalar.dma_start(out=bias_row[0:1, :], in_=qkv2_b.rearrange("(o n) -> o n", o=1))

        load_x(CHUNKS[0])
        load_x(CHUNKS[1])
        load_w(0)
        load_x(CHUNKS[2])
        load_x(CHUNKS[3])
        load_w(1)
        load_w(2)
        for chunk in CHUNKS[4:]:
            load_x(chunk)

        ident = const.tile([P, P], F32, name="ident")
        make_identity(nc, ident[:])
        ident_bf = const.tile([P, P], BF16, name="ident_bf")
        nc.vector.tensor_copy(out=ident_bf[:], in_=ident[:])
        rot = const.tile([P, P], F32, name="rot")
        ident_rows = ident[:].rearrange("k (a b) -> k a b", b=NWS)
        rot_rows = rot[:].rearrange("k (a b) -> k a b", b=NWS)
        nc.vector.tensor_copy(out=rot_rows[:, :, 0 : NWS - 1], in_=ident_rows[:, :, 1:NWS])
        nc.vector.tensor_copy(out=rot_rows[:, :, NWS - 1 : NWS], in_=ident_rows[:, :, 0:1])
        eps = const.tile([P, 1], F32, name="eps")
        nc.vector.memset(eps[:], EPS)
        warm = const.tile([P, 1], F32, name="warm")
        nc.scalar.activation(out=warm[:], in_=eps[:], func=ACT.Sqrt)

        gb_t = psum_t.tile([P, P], BF16, tag="xt")
        nc.tensor.transpose(gb_t[:], gb_rows[:], ident_bf[:])
        gb = const.tile([P, 2 * PACK], F32, name="gb")
        nc.vector.tensor_copy(out=gb[:], in_=gb_t[:, 0 : 2 * PACK])

        ones = const.tile([P, P], BF16, name="ones")
        nc.vector.memset(ones[:], 1.0)
        for s in range(3):
            spread = psum_o.tile([P, D], F32, name="acc")
            nc.tensor.matmul(
                spread[:], lhsT=ones[:], rhs=bias_row[:, D * s : D * s + D], start=True, stop=True
            )
            nc.scalar.copy(out=bias_bc[:, D * s : D * s + D], in_=spread[:])

        w_grouped = keep.tile([P, 3 * D, PACK], BF16, name="w_grouped", align_bytes=64)
        w_codes = keep.tile([P, 3 * D], U32, name="w_codes", align_bytes=64)
        w_scales = keep.tile([P, 3 * D], U8, name="w_scales", align_bytes=64)

        def quantise_w(s):
            cols = slice(D * s, D * s + D)
            for piece in range(4):
                pc = slice(D * s + P * piece, D * s + P * piece + P)
                nc.gpsimd.tensor_scalar(
                    out=w_grouped[:, pc, :],
                    in0=w_raw[:, :, pc].rearrange("q t n -> q n t"),
                    scalar1=1.0,
                    scalar2=0.0,
                    op0=ALU.mult,
                    op1=ALU.add,
                )
            nc.vector.quantize_mx(
                out=w_codes[:, cols].bitcast(FP8X4),
                scales=w_scales[:, cols],
                in_=w_grouped[:, cols, :].rearrange("q n t -> q (n t)"),
            )

        scale_of = {}
        shift_of = {}
        xn_of = {}
        planes_of = {}
        a_codes = {}
        a_scales = {}

        def statistics(chunk):
            x_c = x_tiles[chunk]
            negmean = small.tile([P, WS, 1], F32, name="negmean")
            std = small.tile([P, WS, 1], F32, name="std")
            if chunk in SCALAR_STATS:
                sums = small.tile([P, WS, 1], F32, name="sums")
                squares = small.tile([P, WS, 1], F32, name="squares")
                unread_a = work.tile([P, WS, D], BF16, name="unread_a")
                unread_b = work.tile([P, WS, D], BF16, name="unread_b")
                for j in range(WS):
                    nc.scalar.activation(
                        out=unread_a[:, j, :],
                        in_=x_c[:, j, :],
                        func=ACT.Identity,
                        accum_out=sums[:, j, :],
                    )
                nc.scalar.mul(out=negmean[:], in_=sums[:], mul=-1.0 / D)
                for j in range(WS):
                    nc.scalar.activation(
                        out=unread_b[:, j, :],
                        in_=x_c[:, j, :],
                        func=ACT.Square,
                        bias=negmean[:, j, :],
                        scale=1.0,
                        accum_out=squares[:, j, :],
                    )
                nc.scalar.activation(
                    out=std[:], in_=squares[:], func=ACT.Sqrt, bias=eps[:], scale=1.0 / D
                )
            else:
                stats = small.tile([P, WS, 6], F32, name="stats")
                mv = small.tile([P, WS, 2], F32, name="mv")
                for j in range(WS):
                    nc.vector.bn_stats(out=stats[:, j, :], in_=x_c[:, j, :])
                    nc.vector.bn_aggr(out=mv[:, j, :], in_=stats[:, j, :])
                nc.vector.tensor_scalar_mul(out=negmean[:], in0=mv[:, :, 0:1], scalar1=-1.0)
                nc.scalar.activation(
                    out=std[:], in_=mv[:, :, 1:2], func=ACT.Sqrt, bias=eps[:], scale=1.0
                )
            rstd = small.tile([P, WS, 1], F32, name="rstd")
            nc.vector.reciprocal(out=rstd[:], in_=std[:])
            nmr = small.tile([P, WS, 1], F32, name="nmr")
            nc.vector.tensor_tensor(out=nmr[:], in0=negmean[:], in1=rstd[:], op=ALU.mult)
            scale_of[chunk] = rstd
            shift_of[chunk] = nmr

        def normalise(chunk):
            xn = work.tile([P, WS, D], F32, name="xn")
            for j in range(WS):
                if chunk in VECTOR_NORMALISES:
                    nc.vector.tensor_scalar(
                        out=xn[:, j, :],
                        in0=x_tiles[chunk][:, j, :],
                        scalar1=scale_of[chunk][:, j, :],
                        scalar2=shift_of[chunk][:, j, :],
                        op0=ALU.mult,
                        op1=ALU.add,
                    )
                else:
                    nc.scalar.activation(
                        out=xn[:, j, :],
                        in_=x_tiles[chunk][:, j, :],
                        func=ACT.Identity,
                        scale=scale_of[chunk][:, j, :],
                        bias=shift_of[chunk][:, j, :],
                    )
            xn_of[chunk] = xn

        def transpose_and_scale(chunk):
            xn = xn_of[chunk]
            planes = work.tile([P, PACK, WS * P], BF16, name="planes")
            for t in range(PACK):
                xt = psum_t.tile([P, WS, P], F32, name="xt")
                for j in range(WS):
                    pj = (j + SH) % WS
                    perm = rot if j < SH else ident
                    nc.tensor.transpose(xt[:, pj, :], xn[:, j, P * t : P * t + P], perm[:])
                nc.scalar.activation(
                    out=planes[:, t, :],
                    in_=xt[:].rearrange("q j m -> q (j m)"),
                    func=ACT.Identity,
                    scale=gb[:, t : t + 1],
                    bias=gb[:, PACK + t : PACK + t + 1],
                )
            planes_of[chunk] = planes

        def regroup_and_quantise(chunk):
            grouped = work.tile([P, WS * P, PACK], BF16, name="grouped", align_bytes=64)
            dst = grouped[:].rearrange("q (c i) t -> q c t i", i=4)
            src = planes_of[chunk][:].rearrange("q t (c i) -> q c t i", i=4)
            if chunk in VECTOR_REGROUPS:
                nc.vector.tensor_copy(out=dst, in_=src)
            else:
                nc.scalar.copy(out=dst, in_=src)
            codes = keep.tile([P, WS * P], U32, name="codes_%d_%d" % chunk, align_bytes=64)
            scales = keep.tile([P, WS * P], U8, name="scales_%d_%d" % chunk, align_bytes=64)
            nc.vector.quantize_mx(
                out=codes[:].bitcast(FP8X4),
                scales=scales[:],
                in_=grouped[:].rearrange("q m t -> q (m t)"),
            )
            a_codes[chunk] = codes
            a_scales[chunk] = scales

        def layer_norm(stage):
            for chunk in stage:
                statistics(chunk)
            for chunk in stage:
                normalise(chunk)
                transpose_and_scale(chunk)
                regroup_and_quantise(chunk)

        def project(stage):
            rows = len(stage)
            g, row0 = stage[0]
            blocks_per_store = BANKS_PER_STORE // rows
            heads = HEADS_PER_BLOCK * blocks_per_store
            for blk0 in range(0, BLOCKS, blocks_per_store):
                z = zpool.tile([P, heads, rows * WS, HD], F32, name="z", tag="z")
                for b in range(blocks_per_store):
                    cols = slice(BLOCK * (blk0 + b), BLOCK * (blk0 + b) + BLOCK)
                    bias_view = (
                        bias_bc[:, cols]
                        .rearrange("m (n o c) -> m n o c", n=HEADS_PER_BLOCK, o=1)
                        .to_broadcast([P, HEADS_PER_BLOCK, WS, HD])
                    )
                    for r, chunk in enumerate(stage):
                        acc = psum_o.tile([P, WS, BLOCK], F32, name="acc")
                        for pj in range(WS):
                            toks = slice(P * pj, P * pj + P)
                            nc.tensor.matmul_mx(
                                out=acc[:, pj, :],
                                lhsT=a_codes[chunk][:, toks].bitcast(FP8X4),
                                lhsT_scale=a_scales[chunk][:, toks],
                                rhs=w_codes[:, cols].bitcast(FP8X4),
                                rhs_scale=w_scales[:, cols],
                                start=True,
                                stop=True,
                            )
                        nc.vector.tensor_tensor(
                            out=z[
                                :,
                                HEADS_PER_BLOCK * b : HEADS_PER_BLOCK * (b + 1),
                                WS * r : WS * r + WS,
                                :,
                            ],
                            in0=acc[:].rearrange("m p (n c) -> m n p c", n=HEADS_PER_BLOCK),
                            in1=bias_view,
                            op=ALU.add,
                        )
                which = blk0 // BLOCKS_PER_OUT
                h0 = HEADS_PER_BLOCK * (blk0 % BLOCKS_PER_OUT)
                nc.sync.dma_start(
                    out=outs[which][
                        P * g : P * g + P,
                        h0 : h0 + heads,
                        WS * row0 : WS * (row0 + rows),
                        :,
                    ],
                    in_=z[:],
                )

        layer_norm(STAGES[0])
        quantise_w(0)
        layer_norm(STAGES[1])
        quantise_w(1)
        quantise_w(2)
        layer_norm(STAGES[2])
        project(STAGES[0])
        layer_norm(STAGES[3])
        project(STAGES[1])
        project(STAGES[2])
        project(STAGES[3])
